import numpy as np
import ml_dtypes


def mxq(x, axis, fmt="e4m3"):
    dtype, down = {"e4m3": (ml_dtypes.float8_e4m3fn, 7), "e5m2": (ml_dtypes.float8_e5m2, 14)}[fmt]
    v = np.moveaxis(np.asarray(x, np.float32).astype(ml_dtypes.bfloat16).astype(np.float64), axis, -1)
    blocks = v.reshape(v.shape[:-1] + (-1, 32))
    amax = np.abs(blocks).max(-1, keepdims=True)
    byte = np.maximum(np.where(amax > 0, np.frexp(amax)[1] - 1 + 127, 0) - down, 1)
    scale = np.exp2(byte - 127.0)
    codes = (blocks / scale).astype(np.float32).astype(dtype).astype(np.float64)
    return np.moveaxis((codes * scale).reshape(v.shape), -1, axis)


WIDE = False


def mx_kscale(k):
    if not WIDE:
        return np.ones(k)
    levels = np.array([10, -10, 5, -5, 0])
    a = np.random.permutation(np.resize(levels, k // 512 * 4)).reshape(k // 512, 4)
    idx = np.arange(k)
    return np.exp2(a[idx // 512, idx % 128 // 32])


BF16 = ml_dtypes.bfloat16


def bf(x):
    return np.asarray(x, np.float32).astype(BF16)


def f64(x):
    return np.asarray(x).astype(np.float64)


N, V, DIM, DY, HID, MLP_HID = 2, 1024, 512, 512, 128, 1024


def setup_inputs():
    s = mx_kscale(DY)
    return {"q": bf(np.random.standard_normal((N, V, HID)) * 1.4),
            "k": bf(np.random.standard_normal((N, V, HID)) * 1.4),
            "y": bf(np.random.standard_normal((N, V, DY)) * s),
            "Wv": bf(np.random.standard_normal((DY, DIM)) * 2.0 / np.sqrt(DY) / s[:, None]),
            "x": bf(np.random.standard_normal((N, V, DIM)))}


def reference(q, k, y, Wv, x):
    v = mxq(f64(y), 2, "e4m3") @ mxq(f64(Wv), 0, "e4m3")
    s = f64(q) @ f64(k).transpose(0, 2, 1) * HID ** (-0.5)
    e = np.exp(s - s.max(-1, keepdims=True))
    return f64(x) + (mxq(e, 2, "e4m3") @ mxq(v, 1, "e4m3")) / e.sum(-1, keepdims=True)

@@ -1,0 +1,300 @@
+from contextlib import ExitStack
+
+import concourse.mybir as mybir
+from concourse.masks import make_identity
+
+BF16 = mybir.dt.bfloat16
+F32 = mybir.dt.float32
+U32 = mybir.dt.uint32
+U8 = mybir.dt.uint8
+FP8X4 = mybir.dt.float8_e4m3fn_x4
+ALU = mybir.AluOpType
+ACT = mybir.ActivationFunctionType
+
+P = 128
+PACK = 4
+K_PASS = P * PACK
+BANK = 512
+
+BATCHES, TOKENS, HID, DY, DIM = 2, 1024, 128, 512, 512
+TILES = TOKENS // P
+ALL_TILES = BATCHES * TILES
+KEY_PASSES = TOKENS // K_PASS
+SCALE = HID ** -0.5
+
+LAG_TURN = 1
+LAG_PACK = 2
+LAG_OUT = 3
+
+UNITS = 8
+FAST_STEPS = LAG_OUT
+
+FLOPS = 2 * BATCHES * TOKENS * (DY * DIM + TOKENS * HID + TOKENS * DIM)
+
+
+def units_of_step(n):
+    if -1 <= n < FAST_STEPS:
+        return [(0, 2 * n + 2), (0, 2 * n + 3)]
+    if FAST_STEPS <= n < FAST_STEPS + UNITS:
+        return [(1, n - FAST_STEPS)]
+    return []
+
+
+def tile_block_pa_kernel(tc, q, k, y, Wv, x, out):
+    nc = tc.nc
+    with ExitStack() as ctx:
+        keep = ctx.enter_context(tc.tile_pool(name="keep", bufs=1))
+        ring = ctx.enter_context(tc.tile_pool(name="ring", bufs=4))
+        small = ctx.enter_context(tc.tile_pool(name="small", bufs=6))
+        psum = ctx.enter_context(tc.psum_pool(name="psum", bufs=4))
+
+        ident_bf16 = keep.tile([P, P], BF16)
+        make_identity(nc, ident_bf16[:])
+        ident_f32 = keep.tile([P, P], F32)
+        make_identity(nc, ident_f32[:])
+
+        w_rows = keep.tile([P, PACK * DIM], BF16)
+        k_rows, q_rows, y_rows, x_rows = [], [], [], []
+        for b in range(BATCHES):
+            k_rows.append(keep.tile([P, TILES, HID], BF16, name="k_rows%d" % b))
+            nc.sync.dma_start(out=k_rows[b][:], in_=k[b].rearrange("(j p) h -> p j h", p=P))
+            q_rows.append(keep.tile([P, TILES, HID], BF16, name="q_rows%d" % b))
+            nc.sync.dma_start(out=q_rows[b][:], in_=q[b].rearrange("(j p) h -> p j h", p=P))
+            if b == 0:
+                nc.sync.dma_start(
+                    out=w_rows[:].rearrange("p (u w) -> p u w", u=2),
+                    in_=Wv.rearrange("(u p e) c -> p u (e c)", u=2, e=2),
+                )
+            y_rows.append(keep.tile([P, TILES * DY], BF16, name="y_rows%d" % b))
+            y_dst = y_rows[b][:].rearrange("p (s w) -> p s w", s=4)
+            y_src = y[b].rearrange("(s p e) d -> p s (e d)", s=4, e=2)
+            for g in range(KEY_PASSES):
+                nc.sync.dma_start(out=y_dst[:, 2 * g : 2 * g + 2, :], in_=y_src[:, 2 * g : 2 * g + 2, :])
+        for b in range(BATCHES):
+            x_rows.append(keep.tile([P, TILES, DIM], BF16, name="x_rows%d" % b))
+            nc.sync.dma_start(out=x_rows[b][:], in_=x[b].rearrange("(j p) d -> p j d", p=P))
+
+        w_grouped = keep.tile([P, DIM, PACK], BF16, align_bytes=64)
+        nc.vector.tensor_copy(
+            out=w_grouped[:], in_=w_rows[:].rearrange("p (t c) -> p c t", t=PACK)
+        )
+        w_codes = keep.tile([P, DIM], U32, align_bytes=64)
+        w_scales = keep.tile([P, DIM], U8, align_bytes=64)
+        nc.vector.quantize_mx(
+            out=w_codes[:].bitcast(FP8X4),
+            scales=w_scales[:],
+            in_=w_grouped[:].rearrange("p c t -> p (c t)"),
+        )
+
+        k_cols, q_cols, y_grouped, y_codes, y_scales, v_grouped, v_codes, v_scales = (
+            [], [], [], [], [], [], [], [],
+        )
+        for b in range(BATCHES):
+            k_cols.append(keep.tile([P, TOKENS], BF16, name="k_cols%d" % b))
+            q_cols.append(keep.tile([P, TOKENS], BF16, name="q_cols%d" % b))
+            y_grouped.append(
+                keep.tile([P, TILES * P * PACK], BF16, name="y_grouped%d" % b, align_bytes=64)
+            )
+            y_codes.append(keep.tile([P, TILES * P], U32, name="y_codes%d" % b, align_bytes=64))
+            y_scales.append(keep.tile([P, TILES * P], U8, name="y_scales%d" % b, align_bytes=64))
+            v_grouped.append(
+                keep.tile([P, KEY_PASSES, DIM, PACK], BF16, name="v_grouped%d" % b, align_bytes=64)
+            )
+            v_codes.append(keep.tile([P, KEY_PASSES, DIM], U32, name="v_codes%d" % b, align_bytes=64))
+            v_scales.append(keep.tile([P, KEY_PASSES, DIM], U8, name="v_scales%d" % b, align_bytes=64))
+
+        unit_banks = {}
+
+        def unit_on_tensor(b, u):
+            unit_banks[(b, u)] = []
+            for r in range(2):
+                if u < 2:
+                    rows = (k_rows[b], q_rows[b])[u]
+                    bank = psum.tile([P, 4, P], BF16, tag="work", name="heads_bank")
+                    for j in range(4):
+                        nc.tensor.transpose(bank[:, j, :], rows[:, 4 * r + j, :], ident_bf16[:])
+                elif u < 4:
+                    y_words = y_rows[b][:].bitcast(F32)
+                    first = 4 * (u - 2) + 2 * r
+                    bank = psum.tile([P, 2, 2, P], F32, tag="work", name="y_bank")
+                    for row in range(2):
+                        for half in range(2):
+                            start = (first + row) * (DY // 2) + half * P
+                            nc.tensor.transpose(
+                                bank[:, row, half, :], y_words[:, start : start + P], ident_f32[:]
+                            )
+                else:
+                    g, c = (u - 4) // 2, 2 * ((u - 4) % 2) + r
+                    bank = psum.tile([P, PACK, P], F32, tag="work", name="v_bank")
+                    for t in range(PACK):
+                        tok = slice((4 * g + t) * P, (4 * g + t + 1) * P)
+                        dim = slice(c * P, (c + 1) * P)
+                        nc.tensor.matmul_mx(
+                            out=bank[:, t, :],
+                            lhsT=y_codes[b][:, tok].bitcast(FP8X4),
+                            lhsT_scale=y_scales[b][:, tok],
+                            rhs=w_codes[:, dim].bitcast(FP8X4),
+                            rhs_scale=w_scales[:, dim],
+                            start=True,
+                            stop=True,
+                        )
+                unit_banks[(b, u)].append(bank)
+
+        def unit_copies(b, u):
+            for r in range(2):
+                bank = unit_banks[(b, u)][r]
+                if u < 2:
+                    dst = (k_cols[b], q_cols[b])[u][:, BANK * r : BANK * (r + 1)]
+                    src = bank[:].rearrange("p j t -> p (j t)")
+                elif u < 4:
+                    first = 4 * (u - 2) + 2 * r
+                    words = y_grouped[b][:].bitcast(F32).rearrange("p (n t h) -> p n t h", n=TILES, h=2)
+                    dst = words[:, first : first + 2, :, :]
+                    src = bank[:].rearrange("p n h t -> p n t h")
+                else:
+                    g, c = (u - 4) // 2, 2 * ((u - 4) % 2) + r
+                    dst = v_grouped[b][:, g, c * P : (c + 1) * P, :]
+                    src = bank[:].rearrange("p t d -> p d t")
+                if b == 0 and r == 1:
+                    nc.vector.tensor_copy(out=dst, in_=src)
+                else:
+                    nc.scalar.copy(out=dst, in_=src)
+
+        def unit_quantise(b, u):
+            if u in (2, 3):
+                g = u - 2
+                cols = slice(4 * g * P, 4 * (g + 1) * P)
+                nc.vector.quantize_mx(
+                    out=y_codes[b][:, cols].bitcast(FP8X4),
+                    scales=y_scales[b][:, cols],
+                    in_=y_grouped[b][:, 4 * g * P * PACK : 4 * (g + 1) * P * PACK],
+                )
+            if u in (5, 7):
+                g = (u - 4) // 2
+                nc.vector.quantize_mx(
+                    out=v_codes[b][:, g, :].bitcast(FP8X4),
+                    scales=v_scales[b][:, g, :],
+                    in_=v_grouped[b][:, g, :, :].rearrange("p d t -> p (d t)"),
+                )
+
+        scores, shift, part, total, e_rows, turned, e_codes, e_scales, e_grouped, acc = (
+            {}, {}, {}, {}, {}, {}, {}, {}, {}, {},
+        )
+
+        def score(n):
+            b, i = divmod(n, TILES)
+            scores[n] = []
+            for h in range(2):
+                scores[n].append(psum.tile([P, BANK], F32, tag="scores", name="scores"))
+                nc.tensor.matmul(
+                    out=scores[n][h][:],
+                    lhsT=q_cols[b][:, i * P : (i + 1) * P],
+                    rhs=k_cols[b][:, h * BANK : (h + 1) * BANK],
+                    start=True,
+                    stop=True,
+                )
+
+        def find_peak(n):
+            peak = small.tile([P, 2], F32, tag="peak")
+            for h in range(2):
+                nc.vector.tensor_reduce(
+                    out=peak[:, h : h + 1], in_=scores[n][h][:], axis=mybir.AxisListType.X, op=ALU.max
+                )
+            shift[n] = small.tile([P, 1], F32, tag="shift", name="shift")
+            nc.vector.tensor_scalar(
+                out=shift[n][:], in0=peak[:, 0:1], scalar1=peak[:, 1:2], scalar2=-SCALE,
+                op0=ALU.max, op1=ALU.mult,
+            )
+
+        def exponentiate(n):
+            e_rows[n] = ring.tile([P, TOKENS], BF16, tag="e_rows", name="e_rows")
+            part[n] = small.tile([P, 2], F32, tag="part", name="part")
+            for h in range(2):
+                nc.scalar.activation(
+                    out=e_rows[n][:, h * BANK : (h + 1) * BANK],
+                    in_=scores[n][h][:],
+                    func=ACT.Exp,
+                    bias=shift[n][:],
+                    scale=SCALE,
+                    accum_out=part[n][:, h : h + 1],
+                )
+            total[n] = small.tile([P, 1], F32, tag="total", name="total")
+            nc.gpsimd.tensor_tensor(out=total[n][:], in0=part[n][:, 0:1], in1=part[n][:, 1:2], op=ALU.add)
+
+        def turn(n):
+            e_words = e_rows[n][:].bitcast(F32)
+            turned[n] = psum.tile([P, KEY_PASSES, 2, P], F32, tag="work", name="turned")
+            for g in range(KEY_PASSES):
+                for half in range(2):
+                    start = (2 * g + half) * P
+                    nc.tensor.transpose(
+                        turned[n][:, g, half, :], e_words[:, start : start + P], ident_f32[:]
+                    )
+
+        def pack_copy(n):
+            e_grouped[n] = ring.tile(
+                [P, KEY_PASSES * P * PACK], BF16, tag="e_grouped", name="e_grouped", align_bytes=64
+            )
+            nc.scalar.copy(
+                out=e_grouped[n][:].bitcast(F32).rearrange("p (g r h) -> p g r h", g=KEY_PASSES, h=2),
+                in_=turned[n][:].rearrange("p g h r -> p g r h"),
+            )
+
+        def pack_quantise(n):
+            e_codes[n] = ring.tile([P, KEY_PASSES * P], U32, tag="e_codes", name="e_codes", align_bytes=64)
+            e_scales[n] = ring.tile([P, KEY_PASSES * P], U8, tag="e_scales", name="e_scales", align_bytes=64)
+            nc.vector.quantize_mx(
+                out=e_codes[n][:].bitcast(FP8X4), scales=e_scales[n][:], in_=e_grouped[n][:]
+            )
+
+        def mix(n):
+            b = n // TILES
+            acc[n] = psum.tile([P, DIM], F32, tag="work", name="acc")
+            for g in range(KEY_PASSES):
+                nc.tensor.matmul_mx(
+                    out=acc[n][:],
+                    lhsT=e_codes[n][:, g * P : (g + 1) * P].bitcast(FP8X4),
+                    lhsT_scale=e_scales[n][:, g * P : (g + 1) * P],
+                    rhs=v_codes[b][:, g, :].bitcast(FP8X4),
+                    rhs_scale=v_scales[b][:, g, :],
+                    start=(g == 0),
+                    stop=(g == KEY_PASSES - 1),
+                )
+
+        def finish(n):
+            b, i = divmod(n, TILES)
+            inverse = small.tile([P, 1], F32, tag="inverse")
+            nc.vector.reciprocal(out=inverse[:], in_=total[n][:])
+            result = ring.tile([P, DIM], F32, tag="result")
+            nc.vector.scalar_tensor_tensor(
+                out=result[:], in0=acc[n][:], scalar=inverse[:], in1=x_rows[b][:, i, :],
+                op0=ALU.mult, op1=ALU.add,
+            )
+            nc.sync.dma_start(out=out[b, i * P : (i + 1) * P, :], in_=result[:])
+
+        def is_tile(n):
+            return 0 <= n < ALL_TILES
+
+        for n in range(-2, ALL_TILES + LAG_OUT):
+            if is_tile(n - LAG_OUT):
+                mix(n - LAG_OUT)
+            if is_tile(n - LAG_TURN):
+                turn(n - LAG_TURN)
+            if is_tile(n - LAG_PACK):
+                pack_copy(n - LAG_PACK)
+            if is_tile(n):
+                find_peak(n)
+            for b, u in units_of_step(n):
+                unit_copies(b, u)
+            if is_tile(n):
+                exponentiate(n)
+            if is_tile(n - LAG_OUT):
+                finish(n - LAG_OUT)
+            if is_tile(n - LAG_PACK):
+                pack_quantise(n - LAG_PACK)
+            for b, u in units_of_step(n):
+                unit_quantise(b, u)
+            if is_tile(n + 1):
+                score(n + 1)
+            for b, u in units_of_step(n + 1):
+                unit_on_tensor(b, u)

@@ -155,7 +155,7 @@ def tile_block_pa_kernel(tc, q, k, y, Wv, x, out):
                     g, c = (u - 4) // 2, 2 * ((u - 4) % 2) + r
                     dst = v_grouped[b][:, g, c * P : (c + 1) * P, :]
                     src = bank[:].rearrange("p t d -> p d t")
-                if b == 0 and r == 1:
+                if b == 0 and u >= 4 and r == 1:
                     nc.vector.tensor_copy(out=dst, in_=src)
                 else:
                     nc.scalar.copy(out=dst, in_=src)
@@ -177,9 +177,8 @@ def tile_block_pa_kernel(tc, q, k, y, Wv, x, out):
                     in_=v_grouped[b][:, g, :, :].rearrange("p d t -> p (d t)"),
                 )
 
-        scores, shift, part, total, e_rows, turned, e_codes, e_scales, e_grouped, acc = (
-            {}, {}, {}, {}, {}, {}, {}, {}, {}, {},
-        )
+        scores, peak, shift, part, total, inverse = {}, {}, {}, {}, {}, {}
+        e_rows, turned, e_grouped, e_codes, e_scales, acc = {}, {}, {}, {}, {}, {}
 
         def score(n):
             b, i = divmod(n, TILES)
@@ -194,15 +193,17 @@ def tile_block_pa_kernel(tc, q, k, y, Wv, x, out):
                     stop=True,
                 )
 
-        def find_peak(n):
-            peak = small.tile([P, 2], F32, tag="peak")
+        def find_peaks(n):
+            peak[n] = small.tile([P, 2], F32, tag="peak", name="peak")
             for h in range(2):
                 nc.vector.tensor_reduce(
-                    out=peak[:, h : h + 1], in_=scores[n][h][:], axis=mybir.AxisListType.X, op=ALU.max
+                    out=peak[n][:, h : h + 1], in_=scores[n][h][:], axis=mybir.AxisListType.X, op=ALU.max
                 )
+
+        def find_shift(n):
             shift[n] = small.tile([P, 1], F32, tag="shift", name="shift")
             nc.vector.tensor_scalar(
-                out=shift[n][:], in0=peak[:, 0:1], scalar1=peak[:, 1:2], scalar2=-SCALE,
+                out=shift[n][:], in0=peak[n][:, 0:1], scalar1=peak[n][:, 1:2], scalar2=-SCALE,
                 op0=ALU.max, op1=ALU.mult,
             )
 
@@ -261,13 +262,15 @@ def tile_block_pa_kernel(tc, q, k, y, Wv, x, out):
                     stop=(g == KEY_PASSES - 1),
                 )
 
+        def invert(n):
+            inverse[n] = small.tile([P, 1], F32, tag="inverse", name="inverse")
+            nc.vector.reciprocal(out=inverse[n][:], in_=total[n][:])
+
         def finish(n):
             b, i = divmod(n, TILES)
-            inverse = small.tile([P, 1], F32, tag="inverse")
-            nc.vector.reciprocal(out=inverse[:], in_=total[n][:])
             result = ring.tile([P, DIM], F32, tag="result")
             nc.vector.scalar_tensor_tensor(
-                out=result[:], in0=acc[n][:], scalar=inverse[:], in1=x_rows[b][:, i, :],
+                out=result[:], in0=acc[n][:], scalar=inverse[n][:], in1=x_rows[b][:, i, :],
                 op0=ALU.mult, op1=ALU.add,
             )
             nc.sync.dma_start(out=out[b, i * P : (i + 1) * P, :], in_=result[:])
@@ -275,26 +278,31 @@ def tile_block_pa_kernel(tc, q, k, y, Wv, x, out):
         def is_tile(n):
             return 0 <= n < ALL_TILES
 
-        for n in range(-2, ALL_TILES + LAG_OUT):
-            if is_tile(n - LAG_OUT):
-                mix(n - LAG_OUT)
-            if is_tile(n - LAG_TURN):
-                turn(n - LAG_TURN)
-            if is_tile(n - LAG_PACK):
-                pack_copy(n - LAG_PACK)
-            if is_tile(n):
-                find_peak(n)
-            for b, u in units_of_step(n):
-                unit_copies(b, u)
-            if is_tile(n):
-                exponentiate(n)
-            if is_tile(n - LAG_OUT):
-                finish(n - LAG_OUT)
-            if is_tile(n - LAG_PACK):
-                pack_quantise(n - LAG_PACK)
-            for b, u in units_of_step(n):
-                unit_quantise(b, u)
-            if is_tile(n + 1):
-                score(n + 1)
-            for b, u in units_of_step(n + 1):
-                unit_on_tensor(b, u)
+        with tc.manual_schedule():
+            for n in range(-2, ALL_TILES + LAG_OUT):
+                if is_tile(n - LAG_OUT):
+                    mix(n - LAG_OUT)
+                if is_tile(n - LAG_TURN):
+                    turn(n - LAG_TURN)
+                if is_tile(n - LAG_PACK):
+                    pack_copy(n - LAG_PACK)
+                if is_tile(n):
+                    find_peaks(n)
+                if is_tile(n - LAG_OUT):
+                    invert(n - LAG_OUT)
+                if is_tile(n):
+                    find_shift(n)
+                for b, u in units_of_step(n):
+                    unit_copies(b, u)
+                if is_tile(n):
+                    exponentiate(n)
+                if is_tile(n - LAG_PACK):
+                    pack_quantise(n - LAG_PACK)
+                if is_tile(n - LAG_OUT):
+                    finish(n - LAG_OUT)
+                for b, u in units_of_step(n):
+                    unit_quantise(b, u)
+                if is_tile(n + 1):
+                    score(n + 1)
+                for b, u in units_of_step(n + 1):
+                    unit_on_tensor(b, u)

@@ -57,22 +57,22 @@ def tile_block_pa_kernel(tc, q, k, y, Wv, x, out):
         k_rows, q_rows, y_rows, x_rows = [], [], [], []
         for b in range(BATCHES):
             k_rows.append(keep.tile([P, TILES, HID], BF16, name="k_rows%d" % b))
-            nc.sync.dma_start(out=k_rows[b][:], in_=k[b].rearrange("(j p) h -> p j h", p=P))
+            nc.sync.dma_start(out=k_rows[b][:], in_=k[b].rearrange("(p j) h -> p j h", j=TILES))
             q_rows.append(keep.tile([P, TILES, HID], BF16, name="q_rows%d" % b))
-            nc.sync.dma_start(out=q_rows[b][:], in_=q[b].rearrange("(j p) h -> p j h", p=P))
+            nc.sync.dma_start(out=q_rows[b][:], in_=q[b].rearrange("(p j) h -> p j h", j=TILES))
             if b == 0:
                 nc.sync.dma_start(
                     out=w_rows[:].rearrange("p (u w) -> p u w", u=2),
                     in_=Wv.rearrange("(u p e) c -> p u (e c)", u=2, e=2),
                 )
             y_rows.append(keep.tile([P, TILES * DY], BF16, name="y_rows%d" % b))
-            y_dst = y_rows[b][:].rearrange("p (s w) -> p s w", s=4)
-            y_src = y[b].rearrange("(s p e) d -> p s (e d)", s=4, e=2)
+            y_src = y[b].rearrange("(p j) d -> p (j d)", j=TILES)
             for g in range(KEY_PASSES):
-                nc.sync.dma_start(out=y_dst[:, 2 * g : 2 * g + 2, :], in_=y_src[:, 2 * g : 2 * g + 2, :])
+                cols = slice(g * PACK * DY, (g + 1) * PACK * DY)
+                nc.sync.dma_start(out=y_rows[b][:, cols], in_=y_src[:, cols])
         for b in range(BATCHES):
             x_rows.append(keep.tile([P, TILES, DIM], BF16, name="x_rows%d" % b))
-            nc.sync.dma_start(out=x_rows[b][:], in_=x[b].rearrange("(j p) d -> p j d", p=P))
+            nc.sync.dma_start(out=x_rows[b][:], in_=x[b].rearrange("(p j) d -> p j d", j=TILES))
 
         w_grouped = keep.tile([P, DIM, PACK], BF16, align_bytes=64)
         nc.vector.tensor_copy(
@@ -143,8 +143,11 @@ def tile_block_pa_kernel(tc, q, k, y, Wv, x, out):
         def unit_copies(b, u):
             for r in range(2):
                 bank = unit_banks[(b, u)][r]
-                if u < 2:
-                    dst = (k_cols[b], q_cols[b])[u][:, BANK * r : BANK * (r + 1)]
+                if u == 0:
+                    dst = k_cols[b][:, BANK * r : BANK * (r + 1)].rearrange("p (c t e) -> p c t e", c=2, e=2)
+                    src = bank[:].rearrange("p (c e) t -> p c t e", e=2)
+                elif u == 1:
+                    dst = q_cols[b][:, BANK * r : BANK * (r + 1)]
                     src = bank[:].rearrange("p j t -> p (j t)")
                 elif u < 4:
                     first = 4 * (u - 2) + 2 * r
@@ -273,7 +276,7 @@ def tile_block_pa_kernel(tc, q, k, y, Wv, x, out):
                 out=result[:], in0=acc[n][:], scalar=inverse[n][:], in1=x_rows[b][:, i, :],
                 op0=ALU.mult, op1=ALU.add,
             )
-            nc.sync.dma_start(out=out[b, i * P : (i + 1) * P, :], in_=result[:])
+            nc.sync.dma_start(out=out[b].rearrange("(p j) d -> p j d", j=TILES)[:, i, :], in_=result[:])
 
         def is_tile(n):
             return 0 <= n < ALL_TILES

@@ -24,20 +24,29 @@ SCALE = HID ** -0.5
 
 LAG_TURN = 1
 LAG_PACK = 2
-LAG_OUT = 3
+LAG_OUT = 4
 
-UNITS = 8
-FAST_STEPS = LAG_OUT
+VECTOR_SHARE = {("k", 0, 1), ("q", 0, 1), ("v", 0, 1), ("v", 0, 5), ("v", 1, 1)}
+FIRST_OUT = 5
+GPSIMD_FROM = 2
+W_STEP = 1
+
+BANKS = [("k", 0), ("k", 1), ("q", 0), ("q", 1)] + [("y", r) for r in range(4)] + [("v", r) for r in range(8)]
+PACE = {0: (-1, (4, 2, 2, 4, 4)), 1: (4, (2, 2, 2, 2, 2, 3, 3))}
+
+
+def banks_by_step():
+    plan = {}
+    for b in range(BATCHES):
+        first, counts = PACE[b]
+        done = 0
+        for i, count in enumerate(counts):
+            plan[first + i] = plan.get(first + i, []) + [(b, kind, r) for kind, r in BANKS[done : done + count]]
+            done += count
+    return plan
+
 
 FLOPS = 2 * BATCHES * TOKENS * (DY * DIM + TOKENS * HID + TOKENS * DIM)
-
-
-def units_of_step(n):
-    if -1 <= n < FAST_STEPS:
-        return [(0, 2 * n + 2), (0, 2 * n + 3)]
-    if FAST_STEPS <= n < FAST_STEPS + UNITS:
-        return [(1, n - FAST_STEPS)]
-    return []
 
 
 def tile_block_pa_kernel(tc, q, k, y, Wv, x, out):
@@ -47,6 +56,7 @@ def tile_block_pa_kernel(tc, q, k, y, Wv, x, out):
         ring = ctx.enter_context(tc.tile_pool(name="ring", bufs=4))
         small = ctx.enter_context(tc.tile_pool(name="small", bufs=6))
         psum = ctx.enter_context(tc.psum_pool(name="psum", bufs=4))
+        psc = ctx.enter_context(tc.psum_pool(name="psc", bufs=4))
 
         ident_bf16 = keep.tile([P, P], BF16)
         make_identity(nc, ident_bf16[:])
@@ -60,31 +70,34 @@ def tile_block_pa_kernel(tc, q, k, y, Wv, x, out):
             nc.sync.dma_start(out=k_rows[b][:], in_=k[b].rearrange("(p j) h -> p j h", j=TILES))
             q_rows.append(keep.tile([P, TILES, HID], BF16, name="q_rows%d" % b))
             nc.sync.dma_start(out=q_rows[b][:], in_=q[b].rearrange("(p j) h -> p j h", j=TILES))
-            if b == 0:
-                nc.sync.dma_start(
-                    out=w_rows[:].rearrange("p (u w) -> p u w", u=2),
-                    in_=Wv.rearrange("(u p e) c -> p u (e c)", u=2, e=2),
-                )
             y_rows.append(keep.tile([P, TILES * DY], BF16, name="y_rows%d" % b))
             y_src = y[b].rearrange("(p j) d -> p (j d)", j=TILES)
             for g in range(KEY_PASSES):
                 cols = slice(g * PACK * DY, (g + 1) * PACK * DY)
                 nc.sync.dma_start(out=y_rows[b][:, cols], in_=y_src[:, cols])
+                if b == 0 and g == 0:
+                    nc.sync.dma_start(
+                        out=w_rows[:].rearrange("p (u w) -> p u w", u=2),
+                        in_=Wv.rearrange("(u p e) c -> p u (e c)", u=2, e=2),
+                    )
         for b in range(BATCHES):
             x_rows.append(keep.tile([P, TILES, DIM], BF16, name="x_rows%d" % b))
             nc.sync.dma_start(out=x_rows[b][:], in_=x[b].rearrange("(p j) d -> p j d", j=TILES))
 
         w_grouped = keep.tile([P, DIM, PACK], BF16, align_bytes=64)
-        nc.vector.tensor_copy(
-            out=w_grouped[:], in_=w_rows[:].rearrange("p (t c) -> p c t", t=PACK)
+        nc.gpsimd.tensor_scalar(
+            out=w_grouped[:], in0=w_rows[:].rearrange("p (t c) -> p c t", t=PACK),
+            scalar1=1.0, scalar2=0.0, op0=ALU.mult, op1=ALU.add,
         )
         w_codes = keep.tile([P, DIM], U32, align_bytes=64)
         w_scales = keep.tile([P, DIM], U8, align_bytes=64)
-        nc.vector.quantize_mx(
-            out=w_codes[:].bitcast(FP8X4),
-            scales=w_scales[:],
-            in_=w_grouped[:].rearrange("p c t -> p (c t)"),
-        )
+
+        def w_quantise():
+            nc.vector.quantize_mx(
+                out=w_codes[:].bitcast(FP8X4),
+                scales=w_scales[:],
+                in_=w_grouped[:].rearrange("p c t -> p (c t)"),
+            )
 
         k_cols, q_cols, y_grouped, y_codes, y_scales, v_grouped, v_codes, v_scales = (
             [], [], [], [], [], [], [], [],
@@ -103,77 +116,70 @@ def tile_block_pa_kernel(tc, q, k, y, Wv, x, out):
             v_codes.append(keep.tile([P, KEY_PASSES, DIM], U32, name="v_codes%d" % b, align_bytes=64))
             v_scales.append(keep.tile([P, KEY_PASSES, DIM], U8, name="v_scales%d" % b, align_bytes=64))
 
-        unit_banks = {}
+        banks = {}
 
-        def unit_on_tensor(b, u):
-            unit_banks[(b, u)] = []
-            for r in range(2):
-                if u < 2:
-                    rows = (k_rows[b], q_rows[b])[u]
-                    bank = psum.tile([P, 4, P], BF16, tag="work", name="heads_bank")
-                    for j in range(4):
-                        nc.tensor.transpose(bank[:, j, :], rows[:, 4 * r + j, :], ident_bf16[:])
-                elif u < 4:
-                    y_words = y_rows[b][:].bitcast(F32)
-                    first = 4 * (u - 2) + 2 * r
-                    bank = psum.tile([P, 2, 2, P], F32, tag="work", name="y_bank")
-                    for row in range(2):
-                        for half in range(2):
-                            start = (first + row) * (DY // 2) + half * P
-                            nc.tensor.transpose(
-                                bank[:, row, half, :], y_words[:, start : start + P], ident_f32[:]
-                            )
-                else:
-                    g, c = (u - 4) // 2, 2 * ((u - 4) % 2) + r
-                    bank = psum.tile([P, PACK, P], F32, tag="work", name="v_bank")
-                    for t in range(PACK):
-                        tok = slice((4 * g + t) * P, (4 * g + t + 1) * P)
-                        dim = slice(c * P, (c + 1) * P)
-                        nc.tensor.matmul_mx(
-                            out=bank[:, t, :],
-                            lhsT=y_codes[b][:, tok].bitcast(FP8X4),
-                            lhsT_scale=y_scales[b][:, tok],
-                            rhs=w_codes[:, dim].bitcast(FP8X4),
-                            rhs_scale=w_scales[:, dim],
-                            start=True,
-                            stop=True,
-                        )
-                unit_banks[(b, u)].append(bank)
+        def fill(b, kind, r):
+            if kind in ("k", "q"):
+                rows = k_rows[b] if kind == "k" else q_rows[b]
+                bank = psum.tile([P, 4, P], BF16, tag="work", name="heads_bank")
+                for j in range(4):
+                    nc.tensor.transpose(bank[:, j, :], rows[:, 4 * r + j, :], ident_bf16[:])
+            elif kind == "y":
+                y_words = y_rows[b][:].bitcast(F32)
+                bank = psum.tile([P, 2, 2, P], F32, tag="work", name="y_bank")
+                for row in range(2):
+                    for half in range(2):
+                        start = (2 * r + row) * (DY // 2) + half * P
+                        nc.tensor.transpose(bank[:, row, half, :], y_words[:, start : start + P], ident_f32[:])
+            else:
+                g, c = divmod(r, 4)
+                bank = psum.tile([P, PACK, P], F32, tag="work", name="v_bank")
+                for t in range(PACK):
+                    tok = slice((4 * g + t) * P, (4 * g + t + 1) * P)
+                    dim = slice(c * P, (c + 1) * P)
+                    nc.tensor.matmul_mx(
+                        out=bank[:, t, :],
+                        lhsT=y_codes[b][:, tok].bitcast(FP8X4),
+                        lhsT_scale=y_scales[b][:, tok],
+                        rhs=w_codes[:, dim].bitcast(FP8X4),
+                        rhs_scale=w_scales[:, dim],
+                        start=True,
+                        stop=True,
+                    )
+            banks[(b, kind, r)] = bank
 
-        def unit_copies(b, u):
-            for r in range(2):
-                bank = unit_banks[(b, u)][r]
-                if u == 0:
-                    dst = k_cols[b][:, BANK * r : BANK * (r + 1)].rearrange("p (c t e) -> p c t e", c=2, e=2)
-                    src = bank[:].rearrange("p (c e) t -> p c t e", e=2)
-                elif u == 1:
-                    dst = q_cols[b][:, BANK * r : BANK * (r + 1)]
-                    src = bank[:].rearrange("p j t -> p (j t)")
-                elif u < 4:
-                    first = 4 * (u - 2) + 2 * r
-                    words = y_grouped[b][:].bitcast(F32).rearrange("p (n t h) -> p n t h", n=TILES, h=2)
-                    dst = words[:, first : first + 2, :, :]
-                    src = bank[:].rearrange("p n h t -> p n t h")
-                else:
-                    g, c = (u - 4) // 2, 2 * ((u - 4) % 2) + r
-                    dst = v_grouped[b][:, g, c * P : (c + 1) * P, :]
-                    src = bank[:].rearrange("p t d -> p d t")
-                if b == 0 and u >= 4 and r == 1:
-                    nc.vector.tensor_copy(out=dst, in_=src)
-                else:
-                    nc.scalar.copy(out=dst, in_=src)
+        def empty(b, kind, r):
+            bank = banks[(b, kind, r)]
+            if kind == "k":
+                dst = k_cols[b][:, BANK * r : BANK * (r + 1)].rearrange("p (c t e) -> p c t e", c=2, e=2)
+                src = bank[:].rearrange("p (c e) t -> p c t e", e=2)
+            elif kind == "q":
+                dst = q_cols[b][:, BANK * r : BANK * (r + 1)]
+                src = bank[:].rearrange("p j t -> p (j t)")
+            elif kind == "y":
+                words = y_grouped[b][:].bitcast(F32).rearrange("p (n t h) -> p n t h", n=TILES, h=2)
+                dst = words[:, 2 * r : 2 * r + 2, :, :]
+                src = bank[:].rearrange("p n h t -> p n t h")
+            else:
+                g, c = divmod(r, 4)
+                dst = v_grouped[b][:, g, c * P : (c + 1) * P, :]
+                src = bank[:].rearrange("p t d -> p d t")
+            if (kind, b, r) in VECTOR_SHARE:
+                nc.vector.tensor_copy(out=dst, in_=src)
+            else:
+                nc.scalar.copy(out=dst, in_=src)
 
-        def unit_quantise(b, u):
-            if u in (2, 3):
-                g = u - 2
+        def quantise(b, kind, r):
+            if kind == "y" and r % 2 == 1:
+                g = r // 2
                 cols = slice(4 * g * P, 4 * (g + 1) * P)
                 nc.vector.quantize_mx(
                     out=y_codes[b][:, cols].bitcast(FP8X4),
                     scales=y_scales[b][:, cols],
                     in_=y_grouped[b][:, 4 * g * P * PACK : 4 * (g + 1) * P * PACK],
                 )
-            if u in (5, 7):
-                g = (u - 4) // 2
+            if kind == "v" and r % 4 == 3:
+                g = r // 4
                 nc.vector.quantize_mx(
                     out=v_codes[b][:, g, :].bitcast(FP8X4),
                     scales=v_scales[b][:, g, :],
@@ -187,7 +193,7 @@ def tile_block_pa_kernel(tc, q, k, y, Wv, x, out):
             b, i = divmod(n, TILES)
             scores[n] = []
             for h in range(2):
-                scores[n].append(psum.tile([P, BANK], F32, tag="scores", name="scores"))
+                scores[n].append(psc.tile([P, BANK], F32, tag="scores", name="scores"))
                 nc.tensor.matmul(
                     out=scores[n][h][:],
                     lhsT=q_cols[b][:, i * P : (i + 1) * P],
@@ -205,7 +211,7 @@ def tile_block_pa_kernel(tc, q, k, y, Wv, x, out):
 
         def find_shift(n):
             shift[n] = small.tile([P, 1], F32, tag="shift", name="shift")
-            nc.vector.tensor_scalar(
+            (nc.vector if n < GPSIMD_FROM else nc.gpsimd).tensor_scalar(
                 out=shift[n][:], in0=peak[n][:, 0:1], scalar1=peak[n][:, 1:2], scalar2=-SCALE,
                 op0=ALU.max, op1=ALU.mult,
             )
@@ -281,31 +287,38 @@ def tile_block_pa_kernel(tc, q, k, y, Wv, x, out):
         def is_tile(n):
             return 0 <= n < ALL_TILES
 
+        def out_tiles(n):
+            return [m for m in range(ALL_TILES) if max(m + LAG_OUT, FIRST_OUT) == n]
+
+        plan = banks_by_step()
+
         with tc.manual_schedule():
             for n in range(-2, ALL_TILES + LAG_OUT):
-                if is_tile(n - LAG_OUT):
-                    mix(n - LAG_OUT)
+                outs = out_tiles(n)
+                for m in outs:
+                    mix(m)
                 if is_tile(n - LAG_TURN):
                     turn(n - LAG_TURN)
                 if is_tile(n - LAG_PACK):
                     pack_copy(n - LAG_PACK)
+                for m in outs:
+                    invert(m)
                 if is_tile(n):
                     find_peaks(n)
-                if is_tile(n - LAG_OUT):
-                    invert(n - LAG_OUT)
-                if is_tile(n):
                     find_shift(n)
-                for b, u in units_of_step(n):
-                    unit_copies(b, u)
-                if is_tile(n):
-                    exponentiate(n)
+                for b, kind, r in plan.get(n - 1, []):
+                    quantise(b, kind, r)
+                if n == W_STEP:
+                    w_quantise()
+                for m in outs:
+                    finish(m)
                 if is_tile(n - LAG_PACK):
                     pack_quantise(n - LAG_PACK)
-                if is_tile(n - LAG_OUT):
-                    finish(n - LAG_OUT)
-                for b, u in units_of_step(n):
-                    unit_quantise(b, u)
+                for t in plan.get(n, []):
+                    empty(*t)
+                if is_tile(n):
+                    exponentiate(n)
                 if is_tile(n + 1):
                     score(n + 1)
-                for b, u in units_of_step(n + 1):
-                    unit_on_tensor(b, u)
+                for b, kind, r in plan.get(n + 1, []):
+                    fill(b, kind, r)

@@ -26,9 +26,9 @@ LAG_TURN = 1
 LAG_PACK = 2
 LAG_OUT = 4
 
-VECTOR_SHARE = {("k", 0, 1), ("q", 0, 1), ("v", 0, 1), ("v", 0, 5), ("v", 1, 1)}
+VECTOR_SHARE = {("k", 0, 1), ("q", 0, 1), ("v", 0, 1), ("v", 0, 5)}
 FIRST_OUT = 5
-GPSIMD_FROM = 2
+W_REGROUP_STEP = 0
 W_STEP = 1
 
 BANKS = [("k", 0), ("k", 1), ("q", 0), ("q", 1)] + [("y", r) for r in range(4)] + [("v", r) for r in range(8)]
@@ -85,10 +85,10 @@ def tile_block_pa_kernel(tc, q, k, y, Wv, x, out):
             nc.sync.dma_start(out=x_rows[b][:], in_=x[b].rearrange("(p j) d -> p j d", j=TILES))
 
         w_grouped = keep.tile([P, DIM, PACK], BF16, align_bytes=64)
-        nc.gpsimd.tensor_scalar(
-            out=w_grouped[:], in0=w_rows[:].rearrange("p (t c) -> p c t", t=PACK),
-            scalar1=1.0, scalar2=0.0, op0=ALU.mult, op1=ALU.add,
-        )
+        def w_regroup():
+            nc.vector.tensor_copy(
+                out=w_grouped[:], in_=w_rows[:].rearrange("p (t c) -> p c t", t=PACK)
+            )
         w_codes = keep.tile([P, DIM], U32, align_bytes=64)
         w_scales = keep.tile([P, DIM], U8, align_bytes=64)
 
@@ -211,7 +211,7 @@ def tile_block_pa_kernel(tc, q, k, y, Wv, x, out):
 
         def find_shift(n):
             shift[n] = small.tile([P, 1], F32, tag="shift", name="shift")
-            (nc.vector if n < GPSIMD_FROM else nc.gpsimd).tensor_scalar(
+            nc.vector.tensor_scalar(
                 out=shift[n][:], in0=peak[n][:, 0:1], scalar1=peak[n][:, 1:2], scalar2=-SCALE,
                 op0=ALU.max, op1=ALU.mult,
             )
@@ -301,11 +301,14 @@ def tile_block_pa_kernel(tc, q, k, y, Wv, x, out):
                     turn(n - LAG_TURN)
                 if is_tile(n - LAG_PACK):
                     pack_copy(n - LAG_PACK)
+                if is_tile(n):
+                    find_peaks(n)
                 for m in outs:
                     invert(m)
                 if is_tile(n):
-                    find_peaks(n)
                     find_shift(n)
+                if n == W_REGROUP_STEP:
+                    w_regroup()
                 for b, kind, r in plan.get(n - 1, []):
                     quantise(b, kind, r)
                 if n == W_STEP:

@@ -26,13 +26,13 @@ LAG_TURN = 1
 LAG_PACK = 2
 LAG_OUT = 4
 
-VECTOR_SHARE = {("k", 0, 1), ("q", 0, 1), ("v", 0, 1), ("v", 0, 5)}
+VECTOR_SHARE = {("v", 0, 1), ("v", 0, 3), ("v", 0, 5), ("v", 0, 7)}
 FIRST_OUT = 5
-W_REGROUP_STEP = 0
+W_REGROUP_STEP = -1
 W_STEP = 1
 
 BANKS = [("k", 0), ("k", 1), ("q", 0), ("q", 1)] + [("y", r) for r in range(4)] + [("v", r) for r in range(8)]
-PACE = {0: (-1, (4, 2, 2, 4, 4)), 1: (4, (2, 2, 2, 2, 2, 3, 3))}
+PACE = {0: (-1, (4, 2, 2, 2, 6)), 1: (4, (4, 2, 2, 2, 2, 2, 2))}
 
 
 def banks_by_step():
@@ -70,16 +70,16 @@ def tile_block_pa_kernel(tc, q, k, y, Wv, x, out):
             nc.sync.dma_start(out=k_rows[b][:], in_=k[b].rearrange("(p j) h -> p j h", j=TILES))
             q_rows.append(keep.tile([P, TILES, HID], BF16, name="q_rows%d" % b))
             nc.sync.dma_start(out=q_rows[b][:], in_=q[b].rearrange("(p j) h -> p j h", j=TILES))
+            if b == 0:
+                nc.sync.dma_start(
+                    out=w_rows[:].rearrange("p (u w) -> p u w", u=2),
+                    in_=Wv.rearrange("(u p e) c -> p u (e c)", u=2, e=2),
+                )
             y_rows.append(keep.tile([P, TILES * DY], BF16, name="y_rows%d" % b))
             y_src = y[b].rearrange("(p j) d -> p (j d)", j=TILES)
             for g in range(KEY_PASSES):
                 cols = slice(g * PACK * DY, (g + 1) * PACK * DY)
                 nc.sync.dma_start(out=y_rows[b][:, cols], in_=y_src[:, cols])
-                if b == 0 and g == 0:
-                    nc.sync.dma_start(
-                        out=w_rows[:].rearrange("p (u w) -> p u w", u=2),
-                        in_=Wv.rearrange("(u p e) c -> p u (e c)", u=2, e=2),
-                    )
         for b in range(BATCHES):
             x_rows.append(keep.tile([P, TILES, DIM], BF16, name="x_rows%d" % b))
             nc.sync.dma_start(out=x_rows[b][:], in_=x[b].rearrange("(p j) d -> p j d", j=TILES))
@@ -297,8 +297,6 @@ def tile_block_pa_kernel(tc, q, k, y, Wv, x, out):
                 outs = out_tiles(n)
                 for m in outs:
                     mix(m)
-                if is_tile(n - LAG_TURN):
-                    turn(n - LAG_TURN)
                 if is_tile(n - LAG_PACK):
                     pack_copy(n - LAG_PACK)
                 if is_tile(n):
@@ -323,5 +321,7 @@ def tile_block_pa_kernel(tc, q, k, y, Wv, x, out):
                     exponentiate(n)
                 if is_tile(n + 1):
                     score(n + 1)
+                if is_tile(n - LAG_TURN):
+                    turn(n - LAG_TURN)
                 for b, kind, r in plan.get(n + 1, []):
                     fill(b, kind, r)

@@ -24,15 +24,16 @@ SCALE = HID ** -0.5
 
 LAG_TURN = 1
 LAG_PACK = 2
-LAG_OUT = 4
+LAG_OUT = 5
 
-VECTOR_SHARE = {("v", 0, 1), ("v", 0, 3), ("v", 0, 5), ("v", 0, 7)}
-FIRST_OUT = 5
+VECTOR_SHARE = {("k", 0, 1), ("k", 1, 1), ("q", 1, 1), ("v", 0, 1), ("v", 0, 3), ("v", 0, 5), ("v", 0, 7)}
+PAIRED = 14
+FIRST_OUT = 6
 W_REGROUP_STEP = -1
-W_STEP = 1
+W_STEP = 0
 
 BANKS = [("k", 0), ("k", 1), ("q", 0), ("q", 1)] + [("y", r) for r in range(4)] + [("v", r) for r in range(8)]
-PACE = {0: (-1, (4, 2, 2, 2, 6)), 1: (4, (4, 2, 2, 2, 2, 2, 2))}
+PACE = {0: (-1, (4, 3, 2, 2, 5)), 1: (4, (2,) * 8)}
 
 
 def banks_by_step():
@@ -228,8 +229,11 @@ def tile_block_pa_kernel(tc, q, k, y, Wv, x, out):
                     scale=SCALE,
                     accum_out=part[n][:, h : h + 1],
                 )
-            total[n] = small.tile([P, 1], F32, tag="total", name="total")
-            nc.gpsimd.tensor_tensor(out=total[n][:], in0=part[n][:, 0:1], in1=part[n][:, 1:2], op=ALU.add)
+            if n % 2 == 0:
+                total[n] = total[n + 1] = small.tile([P, 2], F32, tag="total", name="total")
+            nc.gpsimd.tensor_tensor(
+                out=total[n][:, n % 2 : n % 2 + 1], in0=part[n][:, 0:1], in1=part[n][:, 1:2], op=ALU.add
+            )
 
         def turn(n):
             e_words = e_rows[n][:].bitcast(F32)
@@ -241,21 +245,37 @@ def tile_block_pa_kernel(tc, q, k, y, Wv, x, out):
                         turned[n][:, g, half, :], e_words[:, start : start + P], ident_f32[:]
                     )
 
+        def tiles_together(n):
+            return [n - n % 2, n - n % 2 + 1] if n < PAIRED else [n]
+
         def pack_copy(n):
-            e_grouped[n] = ring.tile(
-                [P, KEY_PASSES * P * PACK], BF16, tag="e_grouped", name="e_grouped", align_bytes=64
-            )
+            together = tiles_together(n)
+            if n == together[0]:
+                grouped = ring.tile(
+                    [P, len(together), KEY_PASSES * P * PACK], BF16, tag="e_grouped", name="e_grouped", align_bytes=64
+                )
+                for m in together:
+                    e_grouped[m] = grouped
             nc.scalar.copy(
-                out=e_grouped[n][:].bitcast(F32).rearrange("p (g r h) -> p g r h", g=KEY_PASSES, h=2),
+                out=e_grouped[n][:, n - together[0], :].bitcast(F32).rearrange("p (g r h) -> p g r h", g=KEY_PASSES, h=2),
                 in_=turned[n][:].rearrange("p g h r -> p g r h"),
             )
 
         def pack_quantise(n):
-            e_codes[n] = ring.tile([P, KEY_PASSES * P], U32, tag="e_codes", name="e_codes", align_bytes=64)
-            e_scales[n] = ring.tile([P, KEY_PASSES * P], U8, tag="e_scales", name="e_scales", align_bytes=64)
+            together = tiles_together(n)
+            if n != together[-1]:
+                return
+            width = KEY_PASSES * P
+            codes = ring.tile([P, len(together) * width], U32, tag="e_codes", name="e_codes", align_bytes=64)
+            scales = ring.tile([P, len(together) * width], U8, tag="e_scales", name="e_scales", align_bytes=64)
             nc.vector.quantize_mx(
-                out=e_codes[n][:].bitcast(FP8X4), scales=e_scales[n][:], in_=e_grouped[n][:]
+                out=codes[:].bitcast(FP8X4),
+                scales=scales[:],
+                in_=e_grouped[n][:].rearrange("p m w -> p (m w)"),
             )
+            for i, m in enumerate(together):
+                e_codes[m] = codes[:, i * width : (i + 1) * width]
+                e_scales[m] = scales[:, i * width : (i + 1) * width]
 
         def mix(n):
             b = n // TILES
@@ -272,14 +292,15 @@ def tile_block_pa_kernel(tc, q, k, y, Wv, x, out):
                 )
 
         def invert(n):
-            inverse[n] = small.tile([P, 1], F32, tag="inverse", name="inverse")
-            nc.vector.reciprocal(out=inverse[n][:], in_=total[n][:])
+            if n % 2 == 0:
+                inverse[n] = inverse[n + 1] = small.tile([P, 2], F32, tag="inverse", name="inverse")
+                nc.vector.reciprocal(out=inverse[n][:], in_=total[n][:])
 
         def finish(n):
             b, i = divmod(n, TILES)
             result = ring.tile([P, DIM], F32, tag="result")
             nc.vector.scalar_tensor_tensor(
-                out=result[:], in0=acc[n][:], scalar=inverse[n][:], in1=x_rows[b][:, i, :],
+                out=result[:], in0=acc[n][:], scalar=inverse[n][:, n % 2 : n % 2 + 1], in1=x_rows[b][:, i, :],
                 op0=ALU.mult, op1=ALU.add,
             )
             nc.sync.dma_start(out=out[b].rearrange("(p j) d -> p j d", j=TILES)[:, i, :], in_=result[:])
@@ -303,25 +324,29 @@ def tile_block_pa_kernel(tc, q, k, y, Wv, x, out):
                     find_peaks(n)
                 for m in outs:
                     invert(m)
+                for t in plan.get(n, []):
+                    empty(*t)
                 if is_tile(n):
                     find_shift(n)
                 if n == W_REGROUP_STEP:
                     w_regroup()
-                for b, kind, r in plan.get(n - 1, []):
-                    quantise(b, kind, r)
+                for t in plan.get(n - 1, []):
+                    if t[1] == "v":
+                        quantise(*t)
                 if n == W_STEP:
                     w_quantise()
                 for m in outs:
                     finish(m)
+                for t in plan.get(n, []):
+                    if t[1] == "y":
+                        quantise(*t)
                 if is_tile(n - LAG_PACK):
                     pack_quantise(n - LAG_PACK)
-                for t in plan.get(n, []):
-                    empty(*t)
                 if is_tile(n):
                     exponentiate(n)
-                if is_tile(n + 1):
-                    score(n + 1)
                 if is_tile(n - LAG_TURN):
                     turn(n - LAG_TURN)
-                for b, kind, r in plan.get(n + 1, []):
-                    fill(b, kind, r)
+                if is_tile(n + 1):
+                    score(n + 1)
+                for t in plan.get(n + 1, []):
+                    fill(*t)

@@ -26,14 +26,14 @@ LAG_TURN = 1
 LAG_PACK = 2
 LAG_OUT = 5
 
-VECTOR_SHARE = {("k", 0, 1), ("k", 1, 1), ("q", 1, 1), ("v", 0, 1), ("v", 0, 3), ("v", 0, 5), ("v", 0, 7)}
+VECTOR_SHARE = {("k", 0, 1), ("k", 1, 1), ("q", 1, 1), ("v", 0, 1), ("v", 0, 3), ("v", 0, 5), ("v", 0, 7), ("v", 1, 1)}
 PAIRED = 14
 FIRST_OUT = 6
 W_REGROUP_STEP = -1
 W_STEP = 0
 
 BANKS = [("k", 0), ("k", 1), ("q", 0), ("q", 1)] + [("y", r) for r in range(4)] + [("v", r) for r in range(8)]
-PACE = {0: (-1, (4, 3, 2, 2, 5)), 1: (4, (2,) * 8)}
+PACE = {0: (-1, (4, 2, 2, 2, 2, 4)), 1: (4, (2,) * 8)}
 
 
 def banks_by_step():
@@ -299,17 +299,29 @@ def tile_block_pa_kernel(tc, q, k, y, Wv, x, out):
         def finish(n):
             b, i = divmod(n, TILES)
             result = ring.tile([P, DIM], F32, tag="result")
-            nc.vector.scalar_tensor_tensor(
-                out=result[:], in0=acc[n][:], scalar=inverse[n][:, n % 2 : n % 2 + 1], in1=x_rows[b][:, i, :],
-                op0=ALU.mult, op1=ALU.add,
-            )
-            nc.sync.dma_start(out=out[b].rearrange("(p j) d -> p j d", j=TILES)[:, i, :], in_=result[:])
+            pieces = 2 if n == ALL_TILES - 1 else 1
+            for c in range(pieces):
+                cols = slice(c * DIM // pieces, (c + 1) * DIM // pieces)
+                nc.vector.scalar_tensor_tensor(
+                    out=result[:, cols],
+                    in0=acc[n][:, cols],
+                    scalar=inverse[n][:, n % 2 : n % 2 + 1],
+                    in1=x_rows[b][:, i, cols],
+                    op0=ALU.mult,
+                    op1=ALU.add,
+                )
+                nc.sync.dma_start(
+                    out=out[b].rearrange("(p j) d -> p j d", j=TILES)[:, i, cols], in_=result[:, cols]
+                )
 
         def is_tile(n):
             return 0 <= n < ALL_TILES
 
+        def out_step(m):
+            return m + LAG_PACK + 1 if m >= PAIRED else max(m + LAG_OUT, FIRST_OUT)
+
         def out_tiles(n):
-            return [m for m in range(ALL_TILES) if max(m + LAG_OUT, FIRST_OUT) == n]
+            return [m for m in range(ALL_TILES) if out_step(m) == n]
 
         plan = banks_by_step()
 
@@ -331,22 +343,18 @@ def tile_block_pa_kernel(tc, q, k, y, Wv, x, out):
                 if n == W_REGROUP_STEP:
                     w_regroup()
                 for t in plan.get(n - 1, []):
-                    if t[1] == "v":
-                        quantise(*t)
+                    quantise(*t)
                 if n == W_STEP:
                     w_quantise()
                 for m in outs:
                     finish(m)
-                for t in plan.get(n, []):
-                    if t[1] == "y":
-                        quantise(*t)
                 if is_tile(n - LAG_PACK):
                     pack_quantise(n - LAG_PACK)
                 if is_tile(n):
                     exponentiate(n)
-                if is_tile(n - LAG_TURN):
-                    turn(n - LAG_TURN)
                 if is_tile(n + 1):
                     score(n + 1)
+                if is_tile(n - LAG_TURN):
+                    turn(n - LAG_TURN)
                 for t in plan.get(n + 1, []):
                     fill(*t)

@@ -87,9 +87,10 @@ def tile_block_pa_kernel(tc, q, k, y, Wv, x, out):
 
         w_grouped = keep.tile([P, DIM, PACK], BF16, align_bytes=64)
         def w_regroup():
-            nc.vector.tensor_copy(
-                out=w_grouped[:], in_=w_rows[:].rearrange("p (t c) -> p c t", t=PACK)
-            )
+            by_column = w_rows[:].rearrange("p (t c) -> p c t", t=PACK)
+            half = DIM // 2
+            nc.vector.tensor_copy(out=w_grouped[:, :half, :], in_=by_column[:, :half, :])
+            nc.scalar.copy(out=w_grouped[:, half:, :], in_=by_column[:, half:, :])
         w_codes = keep.tile([P, DIM], U32, align_bytes=64)
         w_scales = keep.tile([P, DIM], U8, align_bytes=64)
 

@@ -26,7 +26,7 @@ LAG_TURN = 1
 LAG_PACK = 2
 LAG_OUT = 5
 
-VECTOR_SHARE = {("k", 0, 1), ("k", 1, 1), ("q", 1, 1), ("v", 0, 1), ("v", 0, 3), ("v", 0, 5), ("v", 0, 7), ("v", 1, 1)}
+VECTOR_SHARE = {("k", 0, 1), ("k", 1, 1), ("q", 1, 1), ("v", 0, 1), ("v", 0, 3), ("v", 0, 5), ("v", 0, 7)}
 PAIRED = 14
 FIRST_OUT = 6
 W_REGROUP_STEP = -1

@@ -26,7 +26,8 @@ LAG_TURN = 1
 LAG_PACK = 2
 LAG_OUT = 5
 
-VECTOR_SHARE = {("k", 0, 1), ("k", 1, 1), ("q", 1, 1), ("v", 0, 1), ("v", 0, 3), ("v", 0, 5), ("v", 0, 7)}
+VECTOR_SHARE = {("k", 0, 1), ("k", 1, 1), ("q", 1, 1), ("v", 0, 1), ("v", 0, 3), ("v", 0, 5), ("v", 0, 7), ("v", 1, 1)}
+INVERTED = 4
 PAIRED = 14
 FIRST_OUT = 6
 W_REGROUP_STEP = -1
@@ -63,6 +64,12 @@ def tile_block_pa_kernel(tc, q, k, y, Wv, x, out):
         make_identity(nc, ident_bf16[:])
         ident_f32 = keep.tile([P, P], F32)
         make_identity(nc, ident_f32[:])
+
+        warm_rows = keep.tile([P, BANK], BF16)
+        nc.vector.memset(warm_rows[:], 0.0)
+        warm_bank = psum.tile([P, BANK], F32, tag="work", name="warm_bank")
+        for i in range(3):
+            nc.tensor.matmul(out=warm_bank[:], lhsT=warm_rows[:, 0:P], rhs=warm_rows[:], start=True, stop=True)
 
         w_rows = keep.tile([P, PACK * DIM], BF16)
         k_rows, q_rows, y_rows, x_rows = [], [], [], []
@@ -213,7 +220,7 @@ def tile_block_pa_kernel(tc, q, k, y, Wv, x, out):
 
         def find_shift(n):
             shift[n] = small.tile([P, 1], F32, tag="shift", name="shift")
-            nc.vector.tensor_scalar(
+            (nc.gpsimd if n >= 6 else nc.vector).tensor_scalar(
                 out=shift[n][:], in0=peak[n][:, 0:1], scalar1=peak[n][:, 1:2], scalar2=-SCALE,
                 op0=ALU.max, op1=ALU.mult,
             )
@@ -230,10 +237,10 @@ def tile_block_pa_kernel(tc, q, k, y, Wv, x, out):
                     scale=SCALE,
                     accum_out=part[n][:, h : h + 1],
                 )
-            if n % 2 == 0:
-                total[n] = total[n + 1] = small.tile([P, 2], F32, tag="total", name="total")
+            i = n % INVERTED
+            total[n] = total[n - 1] if i else small.tile([P, INVERTED], F32, tag="total", name="total")
             nc.gpsimd.tensor_tensor(
-                out=total[n][:, n % 2 : n % 2 + 1], in0=part[n][:, 0:1], in1=part[n][:, 1:2], op=ALU.add
+                out=total[n][:, i : i + 1], in0=part[n][:, 0:1], in1=part[n][:, 1:2], op=ALU.add
             )
 
         def turn(n):
@@ -293,9 +300,11 @@ def tile_block_pa_kernel(tc, q, k, y, Wv, x, out):
                 )
 
         def invert(n):
-            if n % 2 == 0:
-                inverse[n] = inverse[n + 1] = small.tile([P, 2], F32, tag="inverse", name="inverse")
-                nc.vector.reciprocal(out=inverse[n][:], in_=total[n][:])
+            if n % INVERTED == 0:
+                together = small.tile([P, INVERTED], F32, tag="inverse", name="inverse")
+                nc.vector.reciprocal(out=together[:], in_=total[n][:])
+                for i in range(INVERTED):
+                    inverse[n + i] = together[:, i : i + 1]
 
         def finish(n):
             b, i = divmod(n, TILES)
@@ -306,7 +315,7 @@ def tile_block_pa_kernel(tc, q, k, y, Wv, x, out):
                 nc.vector.scalar_tensor_tensor(
                     out=result[:, cols],
                     in0=acc[n][:, cols],
-                    scalar=inverse[n][:, n % 2 : n % 2 + 1],
+                    scalar=inverse[n],
                     in1=x_rows[b][:, i, cols],
                     op0=ALU.mult,
                     op1=ALU.add,
@@ -319,7 +328,7 @@ def tile_block_pa_kernel(tc, q, k, y, Wv, x, out):
             return 0 <= n < ALL_TILES
 
         def out_step(m):
-            return m + LAG_PACK + 1 if m >= PAIRED else max(m + LAG_OUT, FIRST_OUT)
+            return max(m + LAG_OUT, FIRST_OUT)
 
         def out_tiles(n):
             return [m for m in range(ALL_TILES) if out_step(m) == n]
@@ -333,22 +342,22 @@ def tile_block_pa_kernel(tc, q, k, y, Wv, x, out):
                     mix(m)
                 if is_tile(n - LAG_PACK):
                     pack_copy(n - LAG_PACK)
-                if is_tile(n):
-                    find_peaks(n)
                 for m in outs:
                     invert(m)
+                if is_tile(n):
+                    find_peaks(n)
                 for t in plan.get(n, []):
                     empty(*t)
                 if is_tile(n):
                     find_shift(n)
                 if n == W_REGROUP_STEP:
                     w_regroup()
+                for m in outs:
+                    finish(m)
                 for t in plan.get(n - 1, []):
                     quantise(*t)
                 if n == W_STEP:
                     w_quantise()
-                for m in outs:
-                    finish(m)
                 if is_tile(n - LAG_PACK):
                     pack_quantise(n - LAG_PACK)
                 if is_tile(n):

@@ -26,15 +26,15 @@ LAG_TURN = 1
 LAG_PACK = 2
 LAG_OUT = 5
 
-VECTOR_SHARE = {("k", 0, 1), ("k", 1, 1), ("q", 1, 1), ("v", 0, 1), ("v", 0, 3), ("v", 0, 5), ("v", 0, 7), ("v", 1, 1)}
+VECTOR_SHARE = {("k", 0, 1), ("k", 1, 1), ("q", 1, 1), ("v", 0, 1), ("v", 0, 3), ("v", 0, 5), ("v", 1, 1)}
 INVERTED = 4
 PAIRED = 14
-FIRST_OUT = 6
+FIRST_OUT = (6, 15)
 W_REGROUP_STEP = -1
 W_STEP = 0
 
 BANKS = [("k", 0), ("k", 1), ("q", 0), ("q", 1)] + [("y", r) for r in range(4)] + [("v", r) for r in range(8)]
-PACE = {0: (-1, (4, 2, 2, 2, 2, 4)), 1: (4, (2,) * 8)}
+PACE = {0: (-1, (4, 2, 2, 4, 4)), 1: (4, (2, 2, 1, 1, 1, 1, 2, 2, 2, 2))}
 
 
 def banks_by_step():
@@ -328,7 +328,7 @@ def tile_block_pa_kernel(tc, q, k, y, Wv, x, out):
             return 0 <= n < ALL_TILES
 
         def out_step(m):
-            return max(m + LAG_OUT, FIRST_OUT)
+            return max(m + LAG_OUT, FIRST_OUT[m // TILES])
 
         def out_tiles(n):
             return [m for m in range(ALL_TILES) if out_step(m) == n]

from contextlib import ExitStack

import concourse.mybir as mybir
from concourse.masks import make_identity

BF16 = mybir.dt.bfloat16
F32 = mybir.dt.float32
U32 = mybir.dt.uint32
U8 = mybir.dt.uint8
FP8X4 = mybir.dt.float8_e4m3fn_x4
ALU = mybir.AluOpType
ACT = mybir.ActivationFunctionType

P = 128
PACK = 4
K_PASS = P * PACK
BANK = 512

BATCHES, TOKENS, HID, DY, DIM = 2, 1024, 128, 512, 512
TILES = TOKENS // P
ALL_TILES = BATCHES * TILES
KEY_PASSES = TOKENS // K_PASS
SCALE = HID ** -0.5

LAG_TURN = 1
LAG_PACK = 2
LAG_OUT = 5

VECTOR_SHARE = {("k", 0, 1), ("k", 1, 1), ("q", 1, 1), ("v", 0, 1), ("v", 0, 3), ("v", 0, 5), ("v", 1, 1)}
INVERTED = 4
PAIRED = 14
FIRST_OUT = (6, 15)
W_REGROUP_STEP = -1
W_STEP = 0

BANKS = [("k", 0), ("k", 1), ("q", 0), ("q", 1)] + [("y", r) for r in range(4)] + [("v", r) for r in range(8)]
PACE = {0: (-1, (4, 2, 2, 4, 4)), 1: (4, (2, 2, 1, 1, 1, 1, 2, 2, 2, 2))}


def banks_by_step():
    plan = {}
    for b in range(BATCHES):
        first, counts = PACE[b]
        done = 0
        for i, count in enumerate(counts):
            plan[first + i] = plan.get(first + i, []) + [(b, kind, r) for kind, r in BANKS[done : done + count]]
            done += count
    return plan


FLOPS = 2 * BATCHES * TOKENS * (DY * DIM + TOKENS * HID + TOKENS * DIM)


def tile_block_pa_kernel(tc, q, k, y, Wv, x, out):
    nc = tc.nc
    with ExitStack() as ctx:
        keep = ctx.enter_context(tc.tile_pool(name="keep", bufs=1))
        ring = ctx.enter_context(tc.tile_pool(name="ring", bufs=4))
        small = ctx.enter_context(tc.tile_pool(name="small", bufs=6))
        psum = ctx.enter_context(tc.psum_pool(name="psum", bufs=4))
        psc = ctx.enter_context(tc.psum_pool(name="psc", bufs=4))

        ident_bf16 = keep.tile([P, P], BF16)
        make_identity(nc, ident_bf16[:])
        ident_f32 = keep.tile([P, P], F32)
        make_identity(nc, ident_f32[:])

        warm_rows = keep.tile([P, BANK], BF16)
        nc.vector.memset(warm_rows[:], 0.0)
        warm_bank = psum.tile([P, BANK], F32, tag="work", name="warm_bank")
        for i in range(3):
            nc.tensor.matmul(out=warm_bank[:], lhsT=warm_rows[:, 0:P], rhs=warm_rows[:], start=True, stop=True)

        w_rows = keep.tile([P, PACK * DIM], BF16)
        k_rows, q_rows, y_rows, x_rows = [], [], [], []
        for b in range(BATCHES):
            k_rows.append(keep.tile([P, TILES, HID], BF16, name="k_rows%d" % b))
            nc.sync.dma_start(out=k_rows[b][:], in_=k[b].rearrange("(p j) h -> p j h", j=TILES))
            q_rows.append(keep.tile([P, TILES, HID], BF16, name="q_rows%d" % b))
            nc.sync.dma_start(out=q_rows[b][:], in_=q[b].rearrange("(p j) h -> p j h", j=TILES))
            if b == 0:
                nc.sync.dma_start(
                    out=w_rows[:].rearrange("p (u w) -> p u w", u=2),
                    in_=Wv.rearrange("(u p e) c -> p u (e c)", u=2, e=2),
                )
            y_rows.append(keep.tile([P, TILES * DY], BF16, name="y_rows%d" % b))
            y_src = y[b].rearrange("(p j) d -> p (j d)", j=TILES)
            for g in range(KEY_PASSES):
                cols = slice(g * PACK * DY, (g + 1) * PACK * DY)
                nc.sync.dma_start(out=y_rows[b][:, cols], in_=y_src[:, cols])
        for b in range(BATCHES):
            x_rows.append(keep.tile([P, TILES, DIM], BF16, name="x_rows%d" % b))
            nc.sync.dma_start(out=x_rows[b][:], in_=x[b].rearrange("(p j) d -> p j d", j=TILES))

        w_grouped = keep.tile([P, DIM, PACK], BF16, align_bytes=64)
        def w_regroup():
            by_column = w_rows[:].rearrange("p (t c) -> p c t", t=PACK)
            half = DIM // 2
            nc.vector.tensor_copy(out=w_grouped[:, :half, :], in_=by_column[:, :half, :])
            nc.scalar.copy(out=w_grouped[:, half:, :], in_=by_column[:, half:, :])
        w_codes = keep.tile([P, DIM], U32, align_bytes=64)
        w_scales = keep.tile([P, DIM], U8, align_bytes=64)

        def w_quantise():
            nc.vector.quantize_mx(
                out=w_codes[:].bitcast(FP8X4),
                scales=w_scales[:],
                in_=w_grouped[:].rearrange("p c t -> p (c t)"),
            )

        k_cols, q_cols, y_grouped, y_codes, y_scales, v_grouped, v_codes, v_scales = (
            [], [], [], [], [], [], [], [],
        )
        for b in range(BATCHES):
            k_cols.append(keep.tile([P, TOKENS], BF16, name="k_cols%d" % b))
            q_cols.append(keep.tile([P, TOKENS], BF16, name="q_cols%d" % b))
            y_grouped.append(
                keep.tile([P, TILES * P * PACK], BF16, name="y_grouped%d" % b, align_bytes=64)
            )
            y_codes.append(keep.tile([P, TILES * P], U32, name="y_codes%d" % b, align_bytes=64))
            y_scales.append(keep.tile([P, TILES * P], U8, name="y_scales%d" % b, align_bytes=64))
            v_grouped.append(
                keep.tile([P, KEY_PASSES, DIM, PACK], BF16, name="v_grouped%d" % b, align_bytes=64)
            )
            v_codes.append(keep.tile([P, KEY_PASSES, DIM], U32, name="v_codes%d" % b, align_bytes=64))
            v_scales.append(keep.tile([P, KEY_PASSES, DIM], U8, name="v_scales%d" % b, align_bytes=64))

        banks = {}

        def fill(b, kind, r):
            if kind in ("k", "q"):
                rows = k_rows[b] if kind == "k" else q_rows[b]
                bank = psum.tile([P, 4, P], BF16, tag="work", name="heads_bank")
                for j in range(4):
                    nc.tensor.transpose(bank[:, j, :], rows[:, 4 * r + j, :], ident_bf16[:])
            elif kind == "y":
                y_words = y_rows[b][:].bitcast(F32)
                bank = psum.tile([P, 2, 2, P], F32, tag="work", name="y_bank")
                for row in range(2):
                    for half in range(2):
                        start = (2 * r + row) * (DY // 2) + half * P
                        nc.tensor.transpose(bank[:, row, half, :], y_words[:, start : start + P], ident_f32[:])
            else:
                g, c = divmod(r, 4)
                bank = psum.tile([P, PACK, P], F32, tag="work", name="v_bank")
                for t in range(PACK):
                    tok = slice((4 * g + t) * P, (4 * g + t + 1) * P)
                    dim = slice(c * P, (c + 1) * P)
                    nc.tensor.matmul_mx(
                        out=bank[:, t, :],
                        lhsT=y_codes[b][:, tok].bitcast(FP8X4),
                        lhsT_scale=y_scales[b][:, tok],
                        rhs=w_codes[:, dim].bitcast(FP8X4),
                        rhs_scale=w_scales[:, dim],
                        start=True,
                        stop=True,
                    )
            banks[(b, kind, r)] = bank

        def empty(b, kind, r):
            bank = banks[(b, kind, r)]
            if kind == "k":
                dst = k_cols[b][:, BANK * r : BANK * (r + 1)].rearrange("p (c t e) -> p c t e", c=2, e=2)
                src = bank[:].rearrange("p (c e) t -> p c t e", e=2)
            elif kind == "q":
                dst = q_cols[b][:, BANK * r : BANK * (r + 1)]
                src = bank[:].rearrange("p j t -> p (j t)")
            elif kind == "y":
                words = y_grouped[b][:].bitcast(F32).rearrange("p (n t h) -> p n t h", n=TILES, h=2)
                dst = words[:, 2 * r : 2 * r + 2, :, :]
                src = bank[:].rearrange("p n h t -> p n t h")
            else:
                g, c = divmod(r, 4)
                dst = v_grouped[b][:, g, c * P : (c + 1) * P, :]
                src = bank[:].rearrange("p t d -> p d t")
            if (kind, b, r) in VECTOR_SHARE:
                nc.vector.tensor_copy(out=dst, in_=src)
            else:
                nc.scalar.copy(out=dst, in_=src)

        def quantise(b, kind, r):
            if kind == "y" and r % 2 == 1:
                g = r // 2
                cols = slice(4 * g * P, 4 * (g + 1) * P)
                nc.vector.quantize_mx(
                    out=y_codes[b][:, cols].bitcast(FP8X4),
                    scales=y_scales[b][:, cols],
                    in_=y_grouped[b][:, 4 * g * P * PACK : 4 * (g + 1) * P * PACK],
                )
            if kind == "v" and r % 4 == 3:
                g = r // 4
                nc.vector.quantize_mx(
                    out=v_codes[b][:, g, :].bitcast(FP8X4),
                    scales=v_scales[b][:, g, :],
                    in_=v_grouped[b][:, g, :, :].rearrange("p d t -> p (d t)"),
                )

        scores, peak, shift, part, total, inverse = {}, {}, {}, {}, {}, {}
        e_rows, turned, e_grouped, e_codes, e_scales, acc = {}, {}, {}, {}, {}, {}

        def score(n):
            b, i = divmod(n, TILES)
            scores[n] = []
            for h in range(2):
                scores[n].append(psc.tile([P, BANK], F32, tag="scores", name="scores"))
                nc.tensor.matmul(
                    out=scores[n][h][:],
                    lhsT=q_cols[b][:, i * P : (i + 1) * P],
                    rhs=k_cols[b][:, h * BANK : (h + 1) * BANK],
                    start=True,
                    stop=True,
                )

        def find_peaks(n):
            peak[n] = small.tile([P, 2], F32, tag="peak", name="peak")
            for h in range(2):
                nc.vector.tensor_reduce(
                    out=peak[n][:, h : h + 1], in_=scores[n][h][:], axis=mybir.AxisListType.X, op=ALU.max
                )

        def find_shift(n):
            shift[n] = small.tile([P, 1], F32, tag="shift", name="shift")
            (nc.gpsimd if n >= 6 else nc.vector).tensor_scalar(
                out=shift[n][:], in0=peak[n][:, 0:1], scalar1=peak[n][:, 1:2], scalar2=-SCALE,
                op0=ALU.max, op1=ALU.mult,
            )

        def exponentiate(n):
            e_rows[n] = ring.tile([P, TOKENS], BF16, tag="e_rows", name="e_rows")
            part[n] = small.tile([P, 2], F32, tag="part", name="part")
            for h in range(2):
                nc.scalar.activation(
                    out=e_rows[n][:, h * BANK : (h + 1) * BANK],
                    in_=scores[n][h][:],
                    func=ACT.Exp,
                    bias=shift[n][:],
                    scale=SCALE,
                    accum_out=part[n][:, h : h + 1],
                )
            i = n % INVERTED
            total[n] = total[n - 1] if i else small.tile([P, INVERTED], F32, tag="total", name="total")
            nc.gpsimd.tensor_tensor(
                out=total[n][:, i : i + 1], in0=part[n][:, 0:1], in1=part[n][:, 1:2], op=ALU.add
            )

        def turn(n):
            e_words = e_rows[n][:].bitcast(F32)
            turned[n] = psum.tile([P, KEY_PASSES, 2, P], F32, tag="work", name="turned")
            for g in range(KEY_PASSES):
                for half in range(2):
                    start = (2 * g + half) * P
                    nc.tensor.transpose(
                        turned[n][:, g, half, :], e_words[:, start : start + P], ident_f32[:]
                    )

        def tiles_together(n):
            return [n - n % 2, n - n % 2 + 1] if n < PAIRED else [n]

        def pack_copy(n):
            together = tiles_together(n)
            if n == together[0]:
                grouped = ring.tile(
                    [P, len(together), KEY_PASSES * P * PACK], BF16, tag="e_grouped", name="e_grouped", align_bytes=64
                )
                for m in together:
                    e_grouped[m] = grouped
            nc.scalar.copy(
                out=e_grouped[n][:, n - together[0], :].bitcast(F32).rearrange("p (g r h) -> p g r h", g=KEY_PASSES, h=2),
                in_=turned[n][:].rearrange("p g h r -> p g r h"),
            )

        def pack_quantise(n):
            together = tiles_together(n)
            if n != together[-1]:
                return
            width = KEY_PASSES * P
            codes = ring.tile([P, len(together) * width], U32, tag="e_codes", name="e_codes", align_bytes=64)
            scales = ring.tile([P, len(together) * width], U8, tag="e_scales", name="e_scales", align_bytes=64)
            nc.vector.quantize_mx(
                out=codes[:].bitcast(FP8X4),
                scales=scales[:],
                in_=e_grouped[n][:].rearrange("p m w -> p (m w)"),
            )
            for i, m in enumerate(together):
                e_codes[m] = codes[:, i * width : (i + 1) * width]
                e_scales[m] = scales[:, i * width : (i + 1) * width]

        def mix(n):
            b = n // TILES
            acc[n] = psum.tile([P, DIM], F32, tag="work", name="acc")
            for g in range(KEY_PASSES):
                nc.tensor.matmul_mx(
                    out=acc[n][:],
                    lhsT=e_codes[n][:, g * P : (g + 1) * P].bitcast(FP8X4),
                    lhsT_scale=e_scales[n][:, g * P : (g + 1) * P],
                    rhs=v_codes[b][:, g, :].bitcast(FP8X4),
                    rhs_scale=v_scales[b][:, g, :],
                    start=(g == 0),
                    stop=(g == KEY_PASSES - 1),
                )

        def invert(n):
            if n % INVERTED == 0:
                together = small.tile([P, INVERTED], F32, tag="inverse", name="inverse")
                nc.vector.reciprocal(out=together[:], in_=total[n][:])
                for i in range(INVERTED):
                    inverse[n + i] = together[:, i : i + 1]

        def finish(n):
            b, i = divmod(n, TILES)
            result = ring.tile([P, DIM], F32, tag="result")
            pieces = 2 if n == ALL_TILES - 1 else 1
            for c in range(pieces):
                cols = slice(c * DIM // pieces, (c + 1) * DIM // pieces)
                nc.vector.scalar_tensor_tensor(
                    out=result[:, cols],
                    in0=acc[n][:, cols],
                    scalar=inverse[n],
                    in1=x_rows[b][:, i, cols],
                    op0=ALU.mult,
                    op1=ALU.add,
                )
                nc.sync.dma_start(
                    out=out[b].rearrange("(p j) d -> p j d", j=TILES)[:, i, cols], in_=result[:, cols]
                )

        def is_tile(n):
            return 0 <= n < ALL_TILES

        def out_step(m):
            return max(m + LAG_OUT, FIRST_OUT[m // TILES])

        def out_tiles(n):
            return [m for m in range(ALL_TILES) if out_step(m) == n]

        plan = banks_by_step()

        with tc.manual_schedule():
            for n in range(-2, ALL_TILES + LAG_OUT):
                outs = out_tiles(n)
                for m in outs:
                    mix(m)
                if is_tile(n - LAG_PACK):
                    pack_copy(n - LAG_PACK)
                for m in outs:
                    invert(m)
                if is_tile(n):
                    find_peaks(n)
                for t in plan.get(n, []):
                    empty(*t)
                if is_tile(n):
                    find_shift(n)
                if n == W_REGROUP_STEP:
                    w_regroup()
                for m in outs:
                    finish(m)
                for t in plan.get(n - 1, []):
                    quantise(*t)
                if n == W_STEP:
                    w_quantise()
                if is_tile(n - LAG_PACK):
                    pack_quantise(n - LAG_PACK)
                if is_tile(n):
                    exponentiate(n)
                if is_tile(n + 1):
                    score(n + 1)
                if is_tile(n - LAG_TURN):
                    turn(n - LAG_TURN)
                for t in plan.get(n + 1, []):
                    fill(*t)
